import numpy as np
import ml_dtypes


def mxq(x, axis, fmt="e4m3"):
    dtype, down = {"e4m3": (ml_dtypes.float8_e4m3fn, 7), "e5m2": (ml_dtypes.float8_e5m2, 14)}[fmt]
    v = np.moveaxis(np.asarray(x, np.float32).astype(ml_dtypes.bfloat16).astype(np.float64), axis, -1)
    blocks = v.reshape(v.shape[:-1] + (-1, 32))
    amax = np.abs(blocks).max(-1, keepdims=True)
    byte = np.maximum(np.where(amax > 0, np.frexp(amax)[1] - 1 + 127, 0) - down, 1)
    scale = np.exp2(byte - 127.0)
    codes = (blocks / scale).astype(np.float32).astype(dtype).astype(np.float64)
    return np.moveaxis((codes * scale).reshape(v.shape), -1, axis)


WIDE = False


def mx_kscale(k):
    if not WIDE:
        return np.ones(k)
    levels = np.array([10, -10, 5, -5, 0])
    a = np.random.permutation(np.resize(levels, k // 512 * 4)).reshape(k // 512, 4)
    idx = np.arange(k)
    return np.exp2(a[idx // 512, idx % 128 // 32])


BF16 = ml_dtypes.bfloat16


def bf(x):
    return np.asarray(x, np.float32).astype(BF16)


def f64(x):
    return np.asarray(x).astype(np.float64)


B, L, D, T = 256, 32, 1024, 8
F = 2 * D
LN_EPS = 1e-5


def erf(v):
    a = np.minimum(np.abs(v), 6.0)
    term = a.copy()
    total = a.copy()
    for n in range(1, 200):
        term = term * (2.0 * a * a / (2 * n + 1))
        total = total + term
    return np.sign(v) * (2.0 / np.sqrt(np.pi)) * np.exp(-a * a) * total


def gelu_erf(v):
    return 0.5 * v * (1.0 + erf(v / np.sqrt(2.0)))


def setup_inputs():
    s, t = mx_kscale(D), mx_kscale(F)
    counts = np.random.randint(1, T + 1, B)
    counts[0] = T
    target_mask = (np.arange(L)[None, :] < counts[:, None]).astype(np.float64)
    context_mask = 1.0 - target_mask
    context_mask[np.random.random(B) < 0.125] = 0.0
    return {"context_repr": bf(np.random.standard_normal((B, L, D)) * (0.75 * np.sqrt(L)) * s),
            "target_mask": bf(target_mask),
            "context_mask": bf(context_mask),
            "W1": bf(np.random.standard_normal((D, F)) / np.sqrt(D) / s[:, None]),
            "b1": bf(np.random.standard_normal(F) * 0.5),
            "gamma": bf((1.0 + 0.1 * np.random.standard_normal(F)) * t),
            "beta": bf(0.2 * np.random.standard_normal(F) * t),
            "W2": bf(np.random.standard_normal((F, D)) / np.sqrt(F) / t[:, None]),
            "b2": bf(np.random.standard_normal(D) * 0.3),
            "num_targets": T}


def reference(context_repr, target_mask, context_mask, W1, b1, gamma, beta, W2, b2, num_targets):
    ctx_count = f64(context_mask).sum(axis=-1)
    ctx_sum = f64(context_repr).sum(axis=1)
    mean = ctx_sum / np.maximum(ctx_count, 1.0)[:, None]
    mean = np.where((ctx_count > 0)[:, None], mean, 0.0)
    h = gelu_erf((mxq(mean, 1, "e4m3") @ mxq(f64(W1), 0, "e4m3")) + f64(b1))
    mu = h.mean(axis=-1, keepdims=True)
    var = ((h - mu) ** 2).mean(axis=-1, keepdims=True)
    hn = (h - mu) / np.sqrt(var + LN_EPS) * f64(gamma) + f64(beta)
    out = (mxq(hn, 1, "e4m3") @ mxq(f64(W2), 0, "e4m3")) + f64(b2)
    tgt_counts = f64(target_mask).sum(axis=-1)
    valid = np.arange(num_targets)[None, :] < tgt_counts[:, None]
    return np.where(valid[:, :, None], out[:, None, :], 0.0)

@@ -1,0 +1,346 @@
+from contextlib import ExitStack
+
+import concourse.mybir as mybir
+from concourse.masks import make_identity
+
+FLOPS = 2 * 256 * 1024 * 2048 * 2
+
+BF16 = mybir.dt.bfloat16
+F32 = mybir.dt.float32
+U32 = mybir.dt.uint32
+U8 = mybir.dt.uint8
+FP8X4 = mybir.dt.float8_e4m3fn_x4
+ALU = mybir.AluOpType
+ACT = mybir.ActivationFunctionType
+AX = mybir.AxisListType
+
+P = 128
+LN_EPS = 1e-5
+
+B1_OFF = 0
+GAMMA_OFF = 2048
+BETA_OFF = 4096
+B2_OFF = 6144
+
+LOADS = (
+    ("w1", 0), ("c", 0), ("w1", 1), ("c", 1), ("w2", 0), ("c", 2), ("w2", 1), ("c", 3),
+    ("c", 4), ("c", 5), ("c", 6), ("c", 7),
+)
+LD_BUFS = 5
+
+
+def tile_simplepredictor_kernel(
+    tc, context_repr, target_mask, context_mask, W1, b1, gamma, beta, W2, b2, num_targets, out
+):
+    nc = tc.nc
+    T = num_targets
+    with ExitStack() as es:
+        const = es.enter_context(tc.tile_pool(name="const", bufs=1))
+        ld = es.enter_context(tc.tile_pool(name="ld", bufs=LD_BUFS))
+        stage = es.enter_context(tc.tile_pool(name="stage", bufs=3))
+        act = es.enter_context(tc.tile_pool(name="act", bufs=1))
+        small = es.enter_context(tc.tile_pool(name="small", bufs=2))
+        outp = es.enter_context(tc.tile_pool(name="outp", bufs=5))
+        pp_pool = es.enter_context(tc.psum_pool(name="pp", bufs=2))
+        mm_pool = es.enter_context(tc.psum_pool(name="mm", bufs=4))
+        tr_pool = es.enter_context(tc.psum_pool(name="tr", bufs=2))
+
+        w1_v = W1.rearrange("(g h t p) n -> g h p t n", g=2, h=2, t=2, p=P)
+        w2_v = W2.rearrange("(g p t) n -> g p (t n)", g=4, p=P, t=4)
+        ctx_flat = context_repr.flatten_outer_dims()
+        ctx_v2 = ctx_flat.rearrange("(m c p j) d -> m p c (j d)", c=2, p=P, j=2)
+        ctx_v1 = ctx_flat.rearrange("(c p j) d -> c p (j d)", p=P, j=2)
+        out_v = out.rearrange("(t p) j d -> t p (j d)", p=P)
+
+        tiles = {}
+
+        def issue_load(k):
+            kind, i = LOADS[k]
+            tl = ld.tile([P, 8192], BF16, name="ldt", tag="ldt")
+            tiles[k] = tl
+            if kind == "w1":
+                for hh in range(2):
+                    nc.sync.dma_start(
+                        out=tl[:, 4096 * hh:4096 * hh + 4096].rearrange("p (t n) -> p t n", t=2),
+                        in_=w1_v[i, hh],
+                    )
+            elif kind == "w2":
+                for gg in range(2):
+                    nc.sync.dma_start(out=tl[:, 4096 * gg:4096 * gg + 4096], in_=w2_v[2 * i + gg])
+            elif i < 7:
+                for hh in range(2):
+                    nc.sync.dma_start(
+                        out=tl[:, 4096 * hh:4096 * hh + 4096].rearrange("p (c x) -> p c x", c=2),
+                        in_=ctx_v2[2 * i + hh],
+                    )
+            else:
+                for cc in range(4):
+                    nc.sync.dma_start(out=tl[:, 2048 * cc:2048 * cc + 2048], in_=ctx_v1[4 * i + cc])
+
+        for k in range(LD_BUFS):
+            issue_load(k)
+
+        cm = const.tile([P, 2, 32], BF16, name="cm")
+        tm = const.tile([P, 2, 32], BF16, name="tm")
+        nc.scalar.dma_start(out=cm[:], in_=context_mask.rearrange("(t p) l -> p t l", p=P))
+        nc.scalar.dma_start(out=tm[:], in_=target_mask.rearrange("(t p) l -> p t l", p=P))
+        vrows = const.tile([P, P], BF16, name="vrows")
+        nc.vector.memset(vrows[:], 0.0)
+        nc.scalar.dma_start(out=vrows[0:16, :], in_=b1.rearrange("(r c) -> r c", c=P))
+        nc.scalar.dma_start(out=vrows[16:32, :], in_=gamma.rearrange("(r c) -> r c", c=P))
+        nc.scalar.dma_start(out=vrows[32:48, :], in_=beta.rearrange("(r c) -> r c", c=P))
+        nc.scalar.dma_start(out=vrows[48:56, :], in_=b2.rearrange("(r c) -> r c", c=P))
+
+        warm = const.tile([P, 1], F32, name="warm")
+        warm2 = const.tile([P, 1], F32, name="warm2")
+        nc.vector.memset(warm[:], 0.0)
+        nc.scalar.activation(out=warm2[:], in_=warm[:], func=ACT.Gelu)
+
+        ident_bf = const.tile([P, P], BF16, name="ident_bf")
+        make_identity(nc, ident_bf[:])
+        ident_f = const.tile([P, P], F32, name="ident_f")
+        make_identity(nc, ident_f[:])
+        sel_f = const.tile([P, 8], F32, name="sel_f")
+        nc.vector.tensor_reduce(
+            out=sel_f[:], in_=ident_f[:].rearrange("p (n i) -> p n i", i=16), axis=AX.X, op=ALU.add
+        )
+        sel = const.tile([P, 8], BF16, name="sel")
+        nc.vector.tensor_copy(out=sel[:], in_=sel_f[:])
+        neg_half = const.tile([P, 1], F32, name="neg_half")
+        nc.vector.memset(neg_half[:], -0.5)
+        jidx = const.tile([P, T], F32, name="jidx")
+        for j in range(T):
+            nc.vector.memset(jidx[:, j:j + 1], float(j))
+
+        cnt = const.tile([P, 2], F32, name="cnt")
+        nc.vector.tensor_reduce(out=cnt[:], in_=cm[:], axis=AX.X, op=ALU.add)
+        cmax = const.tile([P, 2], F32, name="cmax")
+        nc.vector.tensor_scalar_max(out=cmax[:], in0=cnt[:], scalar1=1.0)
+        rec = const.tile([P, 2], F32, name="rec")
+        nc.vector.reciprocal(out=rec[:], in_=cmax[:])
+        pos = const.tile([P, 2], F32, name="pos")
+        nc.vector.tensor_scalar_min(out=pos[:], in0=cnt[:], scalar1=1.0)
+        inv = const.tile([P, 2], F32, name="inv")
+        nc.vector.tensor_mul(out=inv[:], in0=rec[:], in1=pos[:])
+        ntg = const.tile([P, 2], F32, name="ntg")
+        nc.vector.tensor_reduce(out=ntg[:], in_=tm[:], axis=AX.X, op=ALU.add)
+        valid = const.tile([P, 2, T], F32, name="valid")
+        for t in range(2):
+            nc.vector.tensor_scalar(
+                out=valid[:, t, :], in0=jidx[:], scalar1=ntg[:, t:t + 1], scalar2=None, op0=ALU.is_lt
+            )
+
+        inv_ps = tr_pool.tile([P, 2, P], F32, name="inv_ps", tag="tr")
+        for t in range(2):
+            nc.tensor.transpose(
+                out=inv_ps[:, t, :], in_=inv[:, t:t + 1].to_broadcast([P, P]), identity=ident_f[:]
+            )
+        inv_bc = const.tile([P, 2 * P], F32, name="inv_bc")
+        nc.vector.tensor_copy(out=inv_bc[:], in_=inv_ps[:].rearrange("p t b -> p (t b)"))
+
+        v_ps = tr_pool.tile([P, P], BF16, name="v_ps", tag="tr")
+        nc.tensor.transpose(out=v_ps[:], in_=vrows[:], identity=ident_bf[:])
+        v_t = const.tile([P, P], BF16, name="v_t")
+        nc.vector.tensor_copy(out=v_t[:], in_=v_ps[:])
+        bc = const.tile([P, 7168], BF16, name="bc")
+        for k in range(7):
+            b_ps = tr_pool.tile([P, 1024], BF16, name="b_ps", tag="tr")
+            for i in range(8):
+                r = 8 * k + i
+                nc.tensor.transpose(
+                    out=b_ps[:, P * i:P * i + P],
+                    in_=v_t[:, r:r + 1].to_broadcast([P, P]),
+                    identity=ident_bf[:],
+                )
+            if k % 2 == 0:
+                nc.scalar.copy(out=bc[:, 1024 * k:1024 * k + 1024], in_=b_ps[:])
+            else:
+                nc.vector.tensor_copy(out=bc[:, 1024 * k:1024 * k + 1024], in_=b_ps[:])
+
+        w1c = const.tile([P, 2, 2048], U32, name="w1c", align_bytes=64)
+        w1s = const.tile([P, 2, 2048], U8, name="w1s", align_bytes=64)
+        w2c = const.tile([P, 4, 1024], U32, name="w2c", align_bytes=64)
+        w2s = const.tile([P, 4, 1024], U8, name="w2s", align_bytes=64)
+        unit_count = [0]
+
+        def quantise_unit(src, codes, scales):
+            grouped = stage.tile([P, 512, 4], BF16, name="grouped", tag="grouped", align_bytes=64)
+            dst = grouped[:].rearrange("p (c i) t -> p c t i", i=4)
+            s = src.rearrange("p t (c i) -> p c t i", i=4)
+            if unit_count[0] % 2 == 0:
+                nc.vector.tensor_copy(out=dst, in_=s)
+            else:
+                nc.scalar.copy(out=dst, in_=s)
+            unit_count[0] += 1
+            nc.vector.quantize_mx(
+                out=codes.bitcast(FP8X4), scales=scales, in_=grouped[:].rearrange("p n t -> p (n t)")
+            )
+
+        pooled = {}
+        mcodes = {}
+        mscl = {}
+
+        def pool_tile(i, tl):
+            for cc in range(4):
+                c = 4 * i + cc
+                s, cs = divmod(c, 8)
+                if cs == 0:
+                    pooled[s] = pp_pool.tile([P, 8, 64], F32, name="pooled", tag="pooled")
+                for tp in range(8):
+                    for j in range(2):
+                        o = 2048 * cc + 1024 * j + P * tp
+                        nc.tensor.matmul(
+                            out=pooled[s][:, tp, 8 * cs:8 * cs + 8],
+                            lhsT=tl[:, o:o + P],
+                            rhs=sel[:],
+                            start=(j == 0),
+                            stop=(j == 1),
+                        )
+
+        def finish_subgroup(s):
+            bt, hf = divmod(s, 2)
+            if hf == 0:
+                mcodes[bt] = small.tile([P, 2, P], U32, name="mcodes", tag="mcodes", align_bytes=64)
+                mscl[bt] = small.tile([P, 2, P], U8, name="mscl", tag="mscl", align_bytes=64)
+            mgrp = small.tile([P, 2, 64, 4], BF16, name="mgrp", tag="mgrp", align_bytes=64)
+            nc.vector.tensor_tensor(
+                out=mgrp[:],
+                in0=pooled[s][:].rearrange("p (g t) b -> p g b t", g=2),
+                in1=inv_bc[:, 64 * s:64 * s + 64].unsqueeze(1).unsqueeze(3).to_broadcast([P, 2, 64, 4]),
+                op=ALU.mult,
+            )
+            for g in range(2):
+                nc.vector.quantize_mx(
+                    out=mcodes[bt][:, g, 64 * hf:64 * hf + 64].bitcast(FP8X4),
+                    scales=mscl[bt][:, g, 64 * hf:64 * hf + 64],
+                    in_=mgrp[:, g].rearrange("p b t -> p (b t)"),
+                )
+
+        def mlp(bt):
+            h = act.tile([P, 2048], F32, name="h", tag="h")
+            stats = act.tile([P, 4, 6], F32, name="stats", tag="stats")
+            for nb in range(4):
+                sl = slice(512 * nb, 512 * nb + 512)
+                acc = mm_pool.tile([P, 512], F32, name="acc", tag="acc")
+                for g in range(2):
+                    nc.tensor.matmul_mx(
+                        out=acc[:],
+                        lhsT=mcodes[bt][:, g, :].bitcast(FP8X4),
+                        lhsT_scale=mscl[bt][:, g, :],
+                        rhs=w1c[:, g, sl].bitcast(FP8X4),
+                        rhs_scale=w1s[:, g, sl],
+                        start=(g == 0),
+                        stop=(g == 1),
+                    )
+                nc.vector.tensor_tensor(
+                    out=h[:, sl], in0=acc[:], in1=bc[:, B1_OFF + 512 * nb:B1_OFF + 512 * nb + 512], op=ALU.add
+                )
+                nc.scalar.activation(out=h[:, sl], in_=h[:, sl], func=ACT.Gelu)
+                nc.vector.bn_stats(out=stats[:, nb, :], in_=h[:, sl])
+            mv = act.tile([P, 2], F32, name="mv", tag="mv")
+            nc.vector.bn_aggr(out=mv[:], in_=stats[:].rearrange("p c s -> p (c s)"))
+            ve = act.tile([P, 1], F32, name="ve", tag="ve")
+            nc.vector.tensor_scalar_add(out=ve[:], in0=mv[:, 1:2], scalar1=LN_EPS)
+            rstd = act.tile([P, 1], F32, name="rstd", tag="rstd")
+            nc.gpsimd.tensor_tensor(out=rstd[:], in0=ve[:], in1=neg_half[:], op=ALU.pow)
+
+            hnp = act.tile([P, 4, 4, P], BF16, name="hnp", tag="hnp")
+            hgrp = act.tile([P, 4, P, 4], BF16, name="hgrp", tag="hgrp", align_bytes=64)
+            hcodes = act.tile([P, 4, P], U32, name="hcodes", tag="hcodes", align_bytes=64)
+            hscl = act.tile([P, 4, P], U8, name="hscl", tag="hscl", align_bytes=64)
+            acc2 = []
+            for ob in range(2):
+                a2 = mm_pool.tile([P, 512], F32, name="acc2", tag="acc")
+                acc2.append(a2)
+            for g in range(4):
+                sl = slice(512 * g, 512 * g + 512)
+                u = stage.tile([P, 512], F32, name="u", tag="u")
+                nc.vector.scalar_tensor_tensor(
+                    out=u[:],
+                    in0=h[:, sl],
+                    scalar=mv[:, 0:1],
+                    in1=bc[:, GAMMA_OFF + 512 * g:GAMMA_OFF + 512 * g + 512],
+                    op0=ALU.subtract,
+                    op1=ALU.mult,
+                )
+                nc.vector.scalar_tensor_tensor(
+                    out=hnp[:, g].rearrange("b t p -> b p t"),
+                    in0=u[:].rearrange("b (p t) -> b p t", t=4),
+                    scalar=rstd[:, 0:1],
+                    in1=bc[:, BETA_OFF + 512 * g:BETA_OFF + 512 * g + 512].rearrange("b (p t) -> b p t", t=4),
+                    op0=ALU.mult,
+                    op1=ALU.add,
+                )
+                trp = tr_pool.tile([P, 4, P], BF16, name="trp", tag="tr")
+                for t in range(4):
+                    nc.tensor.transpose(out=trp[:, t, :], in_=hnp[:, g, t, :], identity=ident_bf[:])
+                nc.scalar.copy(out=hgrp[:, g], in_=trp[:].rearrange("p t b -> p b t"))
+                nc.vector.quantize_mx(
+                    out=hcodes[:, g, :].bitcast(FP8X4),
+                    scales=hscl[:, g, :],
+                    in_=hgrp[:, g].rearrange("p b t -> p (b t)"),
+                )
+                for ob in range(2):
+                    nc.tensor.matmul_mx(
+                        out=acc2[ob][:],
+                        lhsT=hcodes[:, g, :].bitcast(FP8X4),
+                        lhsT_scale=hscl[:, g, :],
+                        rhs=w2c[:, g, 512 * ob:512 * ob + 512].bitcast(FP8X4),
+                        rhs_scale=w2s[:, g, 512 * ob:512 * ob + 512],
+                        start=(g == 0),
+                        stop=(g == 3),
+                    )
+            y = act.tile([P, 1024], F32, name="y", tag="y")
+            for ob in range(2):
+                nc.vector.tensor_tensor(
+                    out=y[:, 512 * ob:512 * ob + 512],
+                    in0=acc2[ob][:],
+                    in1=bc[:, B2_OFF + 512 * ob:B2_OFF + 512 * ob + 512],
+                    op=ALU.add,
+                )
+            ots = []
+            for jp in range(4):
+                ot = outp.tile([P, 2, 1024], F32, name="ot", tag="ot")
+                for jj in range(2):
+                    j = 2 * jp + jj
+                    if jp % 2 == 0:
+                        nc.vector.tensor_scalar(
+                            out=ot[:, jj, :], in0=y[:], scalar1=valid[:, bt, j:j + 1], scalar2=None, op0=ALU.mult
+                        )
+                    else:
+                        nc.scalar.activation(out=ot[:, jj, :], in_=y[:], func=ACT.Copy, scale=valid[:, bt, j:j + 1])
+                ots.append(ot)
+            return ots
+
+        def store(bt, ots):
+            for jp in range(4):
+                nc.sync.dma_start(
+                    out=out_v[bt][:, 2048 * jp:2048 * jp + 2048], in_=ots[jp][:].rearrange("p j d -> p (j d)")
+                )
+
+        ots0 = None
+        for k in range(len(LOADS)):
+            kind, i = LOADS[k]
+            tl = tiles[k]
+            if kind == "w1":
+                src = tl[:].rearrange("p (t n) -> p t n", t=4)
+                for nb in range(4):
+                    sl = slice(512 * nb, 512 * nb + 512)
+                    quantise_unit(src[:, :, sl], w1c[:, i, sl], w1s[:, i, sl])
+            elif kind == "w2":
+                src = tl[:].rearrange("p (g t n) -> p g t n", g=2, t=4)
+                for gg in range(2):
+                    for ob in range(2):
+                        sl = slice(512 * ob, 512 * ob + 512)
+                        quantise_unit(src[:, gg, :, sl], w2c[:, 2 * i + gg, sl], w2s[:, 2 * i + gg, sl])
+            else:
+                pool_tile(i, tl)
+                if i % 2 == 1:
+                    finish_subgroup(i // 2)
+                if i == 3:
+                    ots0 = mlp(0)
+            if k + LD_BUFS < len(LOADS):
+                issue_load(k + LD_BUFS)
+        store(0, ots0)
+        ots1 = mlp(1)
+        store(1, ots1)

@@ -23,7 +23,7 @@ BETA_OFF = 4096
 B2_OFF = 6144
 
 LOADS = (
-    ("w1", 0), ("c", 0), ("w1", 1), ("c", 1), ("w2", 0), ("c", 2), ("w2", 1), ("c", 3),
+    ("w1", 0), ("w1", 1), ("c", 0), ("c", 1), ("c", 2), ("c", 3), ("w2", 0), ("w2", 1),
     ("c", 4), ("c", 5), ("c", 6), ("c", 7),
 )
 LD_BUFS = 5
@@ -40,7 +40,7 @@ def tile_simplepredictor_kernel(
         stage = es.enter_context(tc.tile_pool(name="stage", bufs=3))
         act = es.enter_context(tc.tile_pool(name="act", bufs=1))
         small = es.enter_context(tc.tile_pool(name="small", bufs=2))
-        outp = es.enter_context(tc.tile_pool(name="outp", bufs=5))
+        outp = es.enter_context(tc.tile_pool(name="outp", bufs=4))
         pp_pool = es.enter_context(tc.psum_pool(name="pp", bufs=2))
         mm_pool = es.enter_context(tc.psum_pool(name="mm", bufs=4))
         tr_pool = es.enter_context(tc.psum_pool(name="tr", bufs=2))
@@ -164,7 +164,7 @@ def tile_simplepredictor_kernel(
         unit_count = [0]
 
         def quantise_unit(src, codes, scales):
-            grouped = stage.tile([P, 512, 4], BF16, name="grouped", tag="grouped", align_bytes=64)
+            grouped = stage.tile([P, 512, 4], BF16, name="grouped", tag="grouped", align_bytes=64, bufs=6)
             dst = grouped[:].rearrange("p (c i) t -> p c t i", i=4)
             s = src.rearrange("p t (c i) -> p c t i", i=4)
             if unit_count[0] % 2 == 0:
@@ -216,7 +216,7 @@ def tile_simplepredictor_kernel(
                     in_=mgrp[:, g].rearrange("p b t -> p (b t)"),
                 )
 
-        def mlp(bt):
+        def mlp_a(bt):
             h = act.tile([P, 2048], F32, name="h", tag="h")
             stats = act.tile([P, 4, 6], F32, name="stats", tag="stats")
             for nb in range(4):
@@ -248,10 +248,6 @@ def tile_simplepredictor_kernel(
             hgrp = act.tile([P, 4, P, 4], BF16, name="hgrp", tag="hgrp", align_bytes=64)
             hcodes = act.tile([P, 4, P], U32, name="hcodes", tag="hcodes", align_bytes=64)
             hscl = act.tile([P, 4, P], U8, name="hscl", tag="hscl", align_bytes=64)
-            acc2 = []
-            for ob in range(2):
-                a2 = mm_pool.tile([P, 512], F32, name="acc2", tag="acc")
-                acc2.append(a2)
             for g in range(4):
                 sl = slice(512 * g, 512 * g + 512)
                 u = stage.tile([P, 512], F32, name="u", tag="u")
@@ -280,6 +276,14 @@ def tile_simplepredictor_kernel(
                     scales=hscl[:, g, :],
                     in_=hgrp[:, g].rearrange("p b t -> p (b t)"),
                 )
+            return hcodes, hscl
+
+        def mlp_b(bt, hcodes, hscl):
+            acc2 = []
+            for ob in range(2):
+                a2 = mm_pool.tile([P, 512], F32, name="acc2", tag="acc")
+                acc2.append(a2)
+            for g in range(4):
                 for ob in range(2):
                     nc.tensor.matmul_mx(
                         out=acc2[ob][:],
@@ -314,11 +318,17 @@ def tile_simplepredictor_kernel(
 
         def store(bt, ots):
             for jp in range(4):
-                nc.sync.dma_start(
-                    out=out_v[bt][:, 2048 * jp:2048 * jp + 2048], in_=ots[jp][:].rearrange("p j d -> p (j d)")
-                )
+                if bt == 1 and jp == 0:
+                    for jj in range(2):
+                        nc.sync.dma_start(out=out_v[bt][:, 1024 * jj:1024 * jj + 1024], in_=ots[jp][:, jj, :])
+                else:
+                    nc.sync.dma_start(
+                        out=out_v[bt][:, 2048 * jp:2048 * jp + 2048], in_=ots[jp][:].rearrange("p j d -> p (j d)")
+                    )
 
         ots0 = None
+        hc0 = None
+        hs0 = None
         for k in range(len(LOADS)):
             kind, i = LOADS[k]
             tl = tiles[k]
@@ -333,14 +343,17 @@ def tile_simplepredictor_kernel(
                     for ob in range(2):
                         sl = slice(512 * ob, 512 * ob + 512)
                         quantise_unit(src[:, gg, :, sl], w2c[:, 2 * i + gg, sl], w2s[:, 2 * i + gg, sl])
+                if i == 1:
+                    ots0 = mlp_b(0, hc0, hs0)
             else:
                 pool_tile(i, tl)
                 if i % 2 == 1:
                     finish_subgroup(i // 2)
                 if i == 3:
-                    ots0 = mlp(0)
+                    hc0, hs0 = mlp_a(0)
             if k + LD_BUFS < len(LOADS):
                 issue_load(k + LD_BUFS)
         store(0, ots0)
-        ots1 = mlp(1)
+        hc1, hs1 = mlp_a(1)
+        ots1 = mlp_b(1, hc1, hs1)
         store(1, ots1)

@@ -26,7 +26,7 @@ LOADS = (
     ("w1", 0), ("w1", 1), ("c", 0), ("c", 1), ("c", 2), ("c", 3), ("w2", 0), ("w2", 1),
     ("c", 4), ("c", 5), ("c", 6), ("c", 7),
 )
-LD_BUFS = 5
+LD_BUFS = 6
 
 
 def tile_simplepredictor_kernel(
@@ -164,7 +164,7 @@ def tile_simplepredictor_kernel(
         unit_count = [0]
 
         def quantise_unit(src, codes, scales):
-            grouped = stage.tile([P, 512, 4], BF16, name="grouped", tag="grouped", align_bytes=64, bufs=6)
+            grouped = stage.tile([P, 512, 4], BF16, name="grouped", tag="grouped", align_bytes=64, bufs=5)
             dst = grouped[:].rearrange("p (c i) t -> p c t i", i=4)
             s = src.rearrange("p t (c i) -> p c t i", i=4)
             if unit_count[0] % 2 == 0:
@@ -250,9 +250,8 @@ def tile_simplepredictor_kernel(
             hscl = act.tile([P, 4, P], U8, name="hscl", tag="hscl", align_bytes=64)
             for g in range(4):
                 sl = slice(512 * g, 512 * g + 512)
-                u = stage.tile([P, 512], F32, name="u", tag="u")
                 nc.vector.scalar_tensor_tensor(
-                    out=u[:],
+                    out=h[:, sl],
                     in0=h[:, sl],
                     scalar=mv[:, 0:1],
                     in1=bc[:, GAMMA_OFF + 512 * g:GAMMA_OFF + 512 * g + 512],
@@ -261,7 +260,7 @@ def tile_simplepredictor_kernel(
                 )
                 nc.vector.scalar_tensor_tensor(
                     out=hnp[:, g].rearrange("b t p -> b p t"),
-                    in0=u[:].rearrange("b (p t) -> b p t", t=4),
+                    in0=h[:, sl].rearrange("b (p t) -> b p t", t=4),
                     scalar=rstd[:, 0:1],
                     in1=bc[:, BETA_OFF + 512 * g:BETA_OFF + 512 * g + 512].rearrange("b (p t) -> b p t", t=4),
                     op0=ALU.mult,

@@ -26,7 +26,7 @@ LOADS = (
     ("w1", 0), ("w1", 1), ("c", 0), ("c", 1), ("c", 2), ("c", 3), ("w2", 0), ("w2", 1),
     ("c", 4), ("c", 5), ("c", 6), ("c", 7),
 )
-LD_BUFS = 6
+LD_BUFS = 5
 
 
 def tile_simplepredictor_kernel(
@@ -106,8 +106,8 @@ def tile_simplepredictor_kernel(
         )
         sel = const.tile([P, 8], BF16, name="sel")
         nc.vector.tensor_copy(out=sel[:], in_=sel_f[:])
-        neg_half = const.tile([P, 1], F32, name="neg_half")
-        nc.vector.memset(neg_half[:], -0.5)
+        eps_col = const.tile([P, 1], F32, name="eps_col")
+        nc.vector.memset(eps_col[:], LN_EPS)
         jidx = const.tile([P, T], F32, name="jidx")
         for j in range(T):
             nc.vector.memset(jidx[:, j:j + 1], float(j))
@@ -164,7 +164,7 @@ def tile_simplepredictor_kernel(
         unit_count = [0]
 
         def quantise_unit(src, codes, scales):
-            grouped = stage.tile([P, 512, 4], BF16, name="grouped", tag="grouped", align_bytes=64, bufs=5)
+            grouped = stage.tile([P, 512, 4], BF16, name="grouped", tag="grouped", align_bytes=64, bufs=6)
             dst = grouped[:].rearrange("p (c i) t -> p c t i", i=4)
             s = src.rearrange("p t (c i) -> p c t i", i=4)
             if unit_count[0] % 2 == 0:
@@ -239,10 +239,10 @@ def tile_simplepredictor_kernel(
                 nc.vector.bn_stats(out=stats[:, nb, :], in_=h[:, sl])
             mv = act.tile([P, 2], F32, name="mv", tag="mv")
             nc.vector.bn_aggr(out=mv[:], in_=stats[:].rearrange("p c s -> p (c s)"))
-            ve = act.tile([P, 1], F32, name="ve", tag="ve")
-            nc.vector.tensor_scalar_add(out=ve[:], in0=mv[:, 1:2], scalar1=LN_EPS)
+            sd = act.tile([P, 1], F32, name="sd", tag="sd")
+            nc.scalar.activation(out=sd[:], in_=mv[:, 1:2], func=ACT.Sqrt, bias=eps_col[:])
             rstd = act.tile([P, 1], F32, name="rstd", tag="rstd")
-            nc.gpsimd.tensor_tensor(out=rstd[:], in0=ve[:], in1=neg_half[:], op=ALU.pow)
+            nc.vector.reciprocal(out=rstd[:], in_=sd[:])
 
             hnp = act.tile([P, 4, 4, P], BF16, name="hnp", tag="hnp")
             hgrp = act.tile([P, 4, P, 4], BF16, name="hgrp", tag="hgrp", align_bytes=64)
@@ -250,8 +250,9 @@ def tile_simplepredictor_kernel(
             hscl = act.tile([P, 4, P], U8, name="hscl", tag="hscl", align_bytes=64)
             for g in range(4):
                 sl = slice(512 * g, 512 * g + 512)
+                u = stage.tile([P, 512], F32, name="u", tag="u")
                 nc.vector.scalar_tensor_tensor(
-                    out=h[:, sl],
+                    out=u[:],
                     in0=h[:, sl],
                     scalar=mv[:, 0:1],
                     in1=bc[:, GAMMA_OFF + 512 * g:GAMMA_OFF + 512 * g + 512],
@@ -260,7 +261,7 @@ def tile_simplepredictor_kernel(
                 )
                 nc.vector.scalar_tensor_tensor(
                     out=hnp[:, g].rearrange("b t p -> b p t"),
-                    in0=h[:, sl].rearrange("b (p t) -> b p t", t=4),
+                    in0=u[:].rearrange("b (p t) -> b p t", t=4),
                     scalar=rstd[:, 0:1],
                     in1=bc[:, BETA_OFF + 512 * g:BETA_OFF + 512 * g + 512].rearrange("b (p t) -> b p t", t=4),
                     op0=ALU.mult,

@@ -244,7 +244,7 @@ def tile_simplepredictor_kernel(
             rstd = act.tile([P, 1], F32, name="rstd", tag="rstd")
             nc.vector.reciprocal(out=rstd[:], in_=sd[:])
 
-            hnp = act.tile([P, 4, 4, P], BF16, name="hnp", tag="hnp")
+            hnp = act.tile([P, 4, 512], BF16, name="hnp", tag="hnp")
             hgrp = act.tile([P, 4, P, 4], BF16, name="hgrp", tag="hgrp", align_bytes=64)
             hcodes = act.tile([P, 4, P], U32, name="hcodes", tag="hcodes", align_bytes=64)
             hscl = act.tile([P, 4, P], U8, name="hscl", tag="hscl", align_bytes=64)
@@ -260,16 +260,20 @@ def tile_simplepredictor_kernel(
                     op1=ALU.mult,
                 )
                 nc.vector.scalar_tensor_tensor(
-                    out=hnp[:, g].rearrange("b t p -> b p t"),
-                    in0=u[:].rearrange("b (p t) -> b p t", t=4),
+                    out=hnp[:, g, :],
+                    in0=u[:],
                     scalar=rstd[:, 0:1],
-                    in1=bc[:, BETA_OFF + 512 * g:BETA_OFF + 512 * g + 512].rearrange("b (p t) -> b p t", t=4),
+                    in1=bc[:, BETA_OFF + 512 * g:BETA_OFF + 512 * g + 512],
                     op0=ALU.mult,
                     op1=ALU.add,
                 )
                 trp = tr_pool.tile([P, 4, P], BF16, name="trp", tag="tr")
                 for t in range(4):
-                    nc.tensor.transpose(out=trp[:, t, :], in_=hnp[:, g, t, :], identity=ident_bf[:])
+                    nc.tensor.transpose(
+                        out=trp[:, t, :],
+                        in_=hnp[:, g, :].rearrange("b (p t) -> b t p", t=4)[:, t, :],
+                        identity=ident_bf[:],
+                    )
                 nc.scalar.copy(out=hgrp[:, g], in_=trp[:].rearrange("p t b -> p b t"))
                 nc.vector.quantize_mx(
                     out=hcodes[:, g, :].bitcast(FP8X4),

from contextlib import ExitStack

import concourse.mybir as mybir
from concourse.masks import make_identity

FLOPS = 2 * 256 * 1024 * 2048 * 2

BF16 = mybir.dt.bfloat16
F32 = mybir.dt.float32
U32 = mybir.dt.uint32
U8 = mybir.dt.uint8
FP8X4 = mybir.dt.float8_e4m3fn_x4
ALU = mybir.AluOpType
ACT = mybir.ActivationFunctionType
AX = mybir.AxisListType

P = 128
LN_EPS = 1e-5

B1_OFF = 0
GAMMA_OFF = 2048
BETA_OFF = 4096
B2_OFF = 6144

LOADS = (
    ("w1", 0), ("w1", 1), ("c", 0), ("c", 1), ("c", 2), ("c", 3), ("w2", 0), ("w2", 1),
    ("c", 4), ("c", 5), ("c", 6), ("c", 7),
)
LD_BUFS = 5


def tile_simplepredictor_kernel(
    tc, context_repr, target_mask, context_mask, W1, b1, gamma, beta, W2, b2, num_targets, out
):
    nc = tc.nc
    T = num_targets
    with ExitStack() as es:
        const = es.enter_context(tc.tile_pool(name="const", bufs=1))
        ld = es.enter_context(tc.tile_pool(name="ld", bufs=LD_BUFS))
        stage = es.enter_context(tc.tile_pool(name="stage", bufs=3))
        act = es.enter_context(tc.tile_pool(name="act", bufs=1))
        small = es.enter_context(tc.tile_pool(name="small", bufs=2))
        outp = es.enter_context(tc.tile_pool(name="outp", bufs=4))
        pp_pool = es.enter_context(tc.psum_pool(name="pp", bufs=2))
        mm_pool = es.enter_context(tc.psum_pool(name="mm", bufs=4))
        tr_pool = es.enter_context(tc.psum_pool(name="tr", bufs=2))

        w1_v = W1.rearrange("(g h t p) n -> g h p t n", g=2, h=2, t=2, p=P)
        w2_v = W2.rearrange("(g p t) n -> g p (t n)", g=4, p=P, t=4)
        ctx_flat = context_repr.flatten_outer_dims()
        ctx_v2 = ctx_flat.rearrange("(m c p j) d -> m p c (j d)", c=2, p=P, j=2)
        ctx_v1 = ctx_flat.rearrange("(c p j) d -> c p (j d)", p=P, j=2)
        out_v = out.rearrange("(t p) j d -> t p (j d)", p=P)

        tiles = {}

        def issue_load(k):
            kind, i = LOADS[k]
            tl = ld.tile([P, 8192], BF16, name="ldt", tag="ldt")
            tiles[k] = tl
            if kind == "w1":
                for hh in range(2):
                    nc.sync.dma_start(
                        out=tl[:, 4096 * hh:4096 * hh + 4096].rearrange("p (t n) -> p t n", t=2),
                        in_=w1_v[i, hh],
                    )
            elif kind == "w2":
                for gg in range(2):
                    nc.sync.dma_start(out=tl[:, 4096 * gg:4096 * gg + 4096], in_=w2_v[2 * i + gg])
            elif i < 7:
                for hh in range(2):
                    nc.sync.dma_start(
                        out=tl[:, 4096 * hh:4096 * hh + 4096].rearrange("p (c x) -> p c x", c=2),
                        in_=ctx_v2[2 * i + hh],
                    )
            else:
                for cc in range(4):
                    nc.sync.dma_start(out=tl[:, 2048 * cc:2048 * cc + 2048], in_=ctx_v1[4 * i + cc])

        for k in range(LD_BUFS):
            issue_load(k)

        cm = const.tile([P, 2, 32], BF16, name="cm")
        tm = const.tile([P, 2, 32], BF16, name="tm")
        nc.scalar.dma_start(out=cm[:], in_=context_mask.rearrange("(t p) l -> p t l", p=P))
        nc.scalar.dma_start(out=tm[:], in_=target_mask.rearrange("(t p) l -> p t l", p=P))
        vrows = const.tile([P, P], BF16, name="vrows")
        nc.vector.memset(vrows[:], 0.0)
        nc.scalar.dma_start(out=vrows[0:16, :], in_=b1.rearrange("(r c) -> r c", c=P))
        nc.scalar.dma_start(out=vrows[16:32, :], in_=gamma.rearrange("(r c) -> r c", c=P))
        nc.scalar.dma_start(out=vrows[32:48, :], in_=beta.rearrange("(r c) -> r c", c=P))
        nc.scalar.dma_start(out=vrows[48:56, :], in_=b2.rearrange("(r c) -> r c", c=P))

        warm = const.tile([P, 1], F32, name="warm")
        warm2 = const.tile([P, 1], F32, name="warm2")
        nc.vector.memset(warm[:], 0.0)
        nc.scalar.activation(out=warm2[:], in_=warm[:], func=ACT.Gelu)

        ident_bf = const.tile([P, P], BF16, name="ident_bf")
        make_identity(nc, ident_bf[:])
        ident_f = const.tile([P, P], F32, name="ident_f")
        make_identity(nc, ident_f[:])
        sel_f = const.tile([P, 8], F32, name="sel_f")
        nc.vector.tensor_reduce(
            out=sel_f[:], in_=ident_f[:].rearrange("p (n i) -> p n i", i=16), axis=AX.X, op=ALU.add
        )
        sel = const.tile([P, 8], BF16, name="sel")
        nc.vector.tensor_copy(out=sel[:], in_=sel_f[:])
        eps_col = const.tile([P, 1], F32, name="eps_col")
        nc.vector.memset(eps_col[:], LN_EPS)
        jidx = const.tile([P, T], F32, name="jidx")
        for j in range(T):
            nc.vector.memset(jidx[:, j:j + 1], float(j))

        cnt = const.tile([P, 2], F32, name="cnt")
        nc.vector.tensor_reduce(out=cnt[:], in_=cm[:], axis=AX.X, op=ALU.add)
        cmax = const.tile([P, 2], F32, name="cmax")
        nc.vector.tensor_scalar_max(out=cmax[:], in0=cnt[:], scalar1=1.0)
        rec = const.tile([P, 2], F32, name="rec")
        nc.vector.reciprocal(out=rec[:], in_=cmax[:])
        pos = const.tile([P, 2], F32, name="pos")
        nc.vector.tensor_scalar_min(out=pos[:], in0=cnt[:], scalar1=1.0)
        inv = const.tile([P, 2], F32, name="inv")
        nc.vector.tensor_mul(out=inv[:], in0=rec[:], in1=pos[:])
        ntg = const.tile([P, 2], F32, name="ntg")
        nc.vector.tensor_reduce(out=ntg[:], in_=tm[:], axis=AX.X, op=ALU.add)
        valid = const.tile([P, 2, T], F32, name="valid")
        for t in range(2):
            nc.vector.tensor_scalar(
                out=valid[:, t, :], in0=jidx[:], scalar1=ntg[:, t:t + 1], scalar2=None, op0=ALU.is_lt
            )

        inv_ps = tr_pool.tile([P, 2, P], F32, name="inv_ps", tag="tr")
        for t in range(2):
            nc.tensor.transpose(
                out=inv_ps[:, t, :], in_=inv[:, t:t + 1].to_broadcast([P, P]), identity=ident_f[:]
            )
        inv_bc = const.tile([P, 2 * P], F32, name="inv_bc")
        nc.vector.tensor_copy(out=inv_bc[:], in_=inv_ps[:].rearrange("p t b -> p (t b)"))

        v_ps = tr_pool.tile([P, P], BF16, name="v_ps", tag="tr")
        nc.tensor.transpose(out=v_ps[:], in_=vrows[:], identity=ident_bf[:])
        v_t = const.tile([P, P], BF16, name="v_t")
        nc.vector.tensor_copy(out=v_t[:], in_=v_ps[:])
        bc = const.tile([P, 7168], BF16, name="bc")
        for k in range(7):
            b_ps = tr_pool.tile([P, 1024], BF16, name="b_ps", tag="tr")
            for i in range(8):
                r = 8 * k + i
                nc.tensor.transpose(
                    out=b_ps[:, P * i:P * i + P],
                    in_=v_t[:, r:r + 1].to_broadcast([P, P]),
                    identity=ident_bf[:],
                )
            if k % 2 == 0:
                nc.scalar.copy(out=bc[:, 1024 * k:1024 * k + 1024], in_=b_ps[:])
            else:
                nc.vector.tensor_copy(out=bc[:, 1024 * k:1024 * k + 1024], in_=b_ps[:])

        w1c = const.tile([P, 2, 2048], U32, name="w1c", align_bytes=64)
        w1s = const.tile([P, 2, 2048], U8, name="w1s", align_bytes=64)
        w2c = const.tile([P, 4, 1024], U32, name="w2c", align_bytes=64)
        w2s = const.tile([P, 4, 1024], U8, name="w2s", align_bytes=64)
        unit_count = [0]

        def quantise_unit(src, codes, scales):
            grouped = stage.tile([P, 512, 4], BF16, name="grouped", tag="grouped", align_bytes=64, bufs=6)
            dst = grouped[:].rearrange("p (c i) t -> p c t i", i=4)
            s = src.rearrange("p t (c i) -> p c t i", i=4)
            if unit_count[0] % 2 == 0:
                nc.vector.tensor_copy(out=dst, in_=s)
            else:
                nc.scalar.copy(out=dst, in_=s)
            unit_count[0] += 1
            nc.vector.quantize_mx(
                out=codes.bitcast(FP8X4), scales=scales, in_=grouped[:].rearrange("p n t -> p (n t)")
            )

        pooled = {}
        mcodes = {}
        mscl = {}

        def pool_tile(i, tl):
            for cc in range(4):
                c = 4 * i + cc
                s, cs = divmod(c, 8)
                if cs == 0:
                    pooled[s] = pp_pool.tile([P, 8, 64], F32, name="pooled", tag="pooled")
                for tp in range(8):
                    for j in range(2):
                        o = 2048 * cc + 1024 * j + P * tp
                        nc.tensor.matmul(
                            out=pooled[s][:, tp, 8 * cs:8 * cs + 8],
                            lhsT=tl[:, o:o + P],
                            rhs=sel[:],
                            start=(j == 0),
                            stop=(j == 1),
                        )

        def finish_subgroup(s):
            bt, hf = divmod(s, 2)
            if hf == 0:
                mcodes[bt] = small.tile([P, 2, P], U32, name="mcodes", tag="mcodes", align_bytes=64)
                mscl[bt] = small.tile([P, 2, P], U8, name="mscl", tag="mscl", align_bytes=64)
            mgrp = small.tile([P, 2, 64, 4], BF16, name="mgrp", tag="mgrp", align_bytes=64)
            nc.vector.tensor_tensor(
                out=mgrp[:],
                in0=pooled[s][:].rearrange("p (g t) b -> p g b t", g=2),
                in1=inv_bc[:, 64 * s:64 * s + 64].unsqueeze(1).unsqueeze(3).to_broadcast([P, 2, 64, 4]),
                op=ALU.mult,
            )
            for g in range(2):
                nc.vector.quantize_mx(
                    out=mcodes[bt][:, g, 64 * hf:64 * hf + 64].bitcast(FP8X4),
                    scales=mscl[bt][:, g, 64 * hf:64 * hf + 64],
                    in_=mgrp[:, g].rearrange("p b t -> p (b t)"),
                )

        def mlp_a(bt):
            h = act.tile([P, 2048], F32, name="h", tag="h")
            stats = act.tile([P, 4, 6], F32, name="stats", tag="stats")
            for nb in range(4):
                sl = slice(512 * nb, 512 * nb + 512)
                acc = mm_pool.tile([P, 512], F32, name="acc", tag="acc")
                for g in range(2):
                    nc.tensor.matmul_mx(
                        out=acc[:],
                        lhsT=mcodes[bt][:, g, :].bitcast(FP8X4),
                        lhsT_scale=mscl[bt][:, g, :],
                        rhs=w1c[:, g, sl].bitcast(FP8X4),
                        rhs_scale=w1s[:, g, sl],
                        start=(g == 0),
                        stop=(g == 1),
                    )
                nc.vector.tensor_tensor(
                    out=h[:, sl], in0=acc[:], in1=bc[:, B1_OFF + 512 * nb:B1_OFF + 512 * nb + 512], op=ALU.add
                )
                nc.scalar.activation(out=h[:, sl], in_=h[:, sl], func=ACT.Gelu)
                nc.vector.bn_stats(out=stats[:, nb, :], in_=h[:, sl])
            mv = act.tile([P, 2], F32, name="mv", tag="mv")
            nc.vector.bn_aggr(out=mv[:], in_=stats[:].rearrange("p c s -> p (c s)"))
            sd = act.tile([P, 1], F32, name="sd", tag="sd")
            nc.scalar.activation(out=sd[:], in_=mv[:, 1:2], func=ACT.Sqrt, bias=eps_col[:])
            rstd = act.tile([P, 1], F32, name="rstd", tag="rstd")
            nc.vector.reciprocal(out=rstd[:], in_=sd[:])

            hnp = act.tile([P, 4, 512], BF16, name="hnp", tag="hnp")
            hgrp = act.tile([P, 4, P, 4], BF16, name="hgrp", tag="hgrp", align_bytes=64)
            hcodes = act.tile([P, 4, P], U32, name="hcodes", tag="hcodes", align_bytes=64)
            hscl = act.tile([P, 4, P], U8, name="hscl", tag="hscl", align_bytes=64)
            for g in range(4):
                sl = slice(512 * g, 512 * g + 512)
                u = stage.tile([P, 512], F32, name="u", tag="u")
                nc.vector.scalar_tensor_tensor(
                    out=u[:],
                    in0=h[:, sl],
                    scalar=mv[:, 0:1],
                    in1=bc[:, GAMMA_OFF + 512 * g:GAMMA_OFF + 512 * g + 512],
                    op0=ALU.subtract,
                    op1=ALU.mult,
                )
                nc.vector.scalar_tensor_tensor(
                    out=hnp[:, g, :],
                    in0=u[:],
                    scalar=rstd[:, 0:1],
                    in1=bc[:, BETA_OFF + 512 * g:BETA_OFF + 512 * g + 512],
                    op0=ALU.mult,
                    op1=ALU.add,
                )
                trp = tr_pool.tile([P, 4, P], BF16, name="trp", tag="tr")
                for t in range(4):
                    nc.tensor.transpose(
                        out=trp[:, t, :],
                        in_=hnp[:, g, :].rearrange("b (p t) -> b t p", t=4)[:, t, :],
                        identity=ident_bf[:],
                    )
                nc.scalar.copy(out=hgrp[:, g], in_=trp[:].rearrange("p t b -> p b t"))
                nc.vector.quantize_mx(
                    out=hcodes[:, g, :].bitcast(FP8X4),
                    scales=hscl[:, g, :],
                    in_=hgrp[:, g].rearrange("p b t -> p (b t)"),
                )
            return hcodes, hscl

        def mlp_b(bt, hcodes, hscl):
            acc2 = []
            for ob in range(2):
                a2 = mm_pool.tile([P, 512], F32, name="acc2", tag="acc")
                acc2.append(a2)
            for g in range(4):
                for ob in range(2):
                    nc.tensor.matmul_mx(
                        out=acc2[ob][:],
                        lhsT=hcodes[:, g, :].bitcast(FP8X4),
                        lhsT_scale=hscl[:, g, :],
                        rhs=w2c[:, g, 512 * ob:512 * ob + 512].bitcast(FP8X4),
                        rhs_scale=w2s[:, g, 512 * ob:512 * ob + 512],
                        start=(g == 0),
                        stop=(g == 3),
                    )
            y = act.tile([P, 1024], F32, name="y", tag="y")
            for ob in range(2):
                nc.vector.tensor_tensor(
                    out=y[:, 512 * ob:512 * ob + 512],
                    in0=acc2[ob][:],
                    in1=bc[:, B2_OFF + 512 * ob:B2_OFF + 512 * ob + 512],
                    op=ALU.add,
                )
            ots = []
            for jp in range(4):
                ot = outp.tile([P, 2, 1024], F32, name="ot", tag="ot")
                for jj in range(2):
                    j = 2 * jp + jj
                    if jp % 2 == 0:
                        nc.vector.tensor_scalar(
                            out=ot[:, jj, :], in0=y[:], scalar1=valid[:, bt, j:j + 1], scalar2=None, op0=ALU.mult
                        )
                    else:
                        nc.scalar.activation(out=ot[:, jj, :], in_=y[:], func=ACT.Copy, scale=valid[:, bt, j:j + 1])
                ots.append(ot)
            return ots

        def store(bt, ots):
            for jp in range(4):
                if bt == 1 and jp == 0:
                    for jj in range(2):
                        nc.sync.dma_start(out=out_v[bt][:, 1024 * jj:1024 * jj + 1024], in_=ots[jp][:, jj, :])
                else:
                    nc.sync.dma_start(
                        out=out_v[bt][:, 2048 * jp:2048 * jp + 2048], in_=ots[jp][:].rearrange("p j d -> p (j d)")
                    )

        ots0 = None
        hc0 = None
        hs0 = None
        for k in range(len(LOADS)):
            kind, i = LOADS[k]
            tl = tiles[k]
            if kind == "w1":
                src = tl[:].rearrange("p (t n) -> p t n", t=4)
                for nb in range(4):
                    sl = slice(512 * nb, 512 * nb + 512)
                    quantise_unit(src[:, :, sl], w1c[:, i, sl], w1s[:, i, sl])
            elif kind == "w2":
                src = tl[:].rearrange("p (g t n) -> p g t n", g=2, t=4)
                for gg in range(2):
                    for ob in range(2):
                        sl = slice(512 * ob, 512 * ob + 512)
                        quantise_unit(src[:, gg, :, sl], w2c[:, 2 * i + gg, sl], w2s[:, 2 * i + gg, sl])
                if i == 1:
                    ots0 = mlp_b(0, hc0, hs0)
            else:
                pool_tile(i, tl)
                if i % 2 == 1:
                    finish_subgroup(i // 2)
                if i == 3:
                    hc0, hs0 = mlp_a(0)
            if k + LD_BUFS < len(LOADS):
                issue_load(k + LD_BUFS)
        store(0, ots0)
        hc1, hs1 = mlp_a(1)
        ots1 = mlp_b(1, hc1, hs1)
        store(1, ots1)
